import numpy as np
import ml_dtypes


def mxq(x, axis, fmt="e4m3"):
    dtype, down = {"e4m3": (ml_dtypes.float8_e4m3fn, 7), "e5m2": (ml_dtypes.float8_e5m2, 14)}[fmt]
    v = np.moveaxis(np.asarray(x, np.float32).astype(ml_dtypes.bfloat16).astype(np.float64), axis, -1)
    blocks = v.reshape(v.shape[:-1] + (-1, 32))
    amax = np.abs(blocks).max(-1, keepdims=True)
    byte = np.maximum(np.where(amax > 0, np.frexp(amax)[1] - 1 + 127, 0) - down, 1)
    scale = np.exp2(byte - 127.0)
    codes = (blocks / scale).astype(np.float32).astype(dtype).astype(np.float64)
    return np.moveaxis((codes * scale).reshape(v.shape), -1, axis)


WIDE = False


def mx_kscale(k):
    if not WIDE:
        return np.ones(k)
    levels = np.array([10, -10, 5, -5, 0])
    a = np.random.permutation(np.resize(levels, k // 512 * 4)).reshape(k // 512, 4)
    idx = np.arange(k)
    return np.exp2(a[idx // 512, idx % 128 // 32])


BF16 = ml_dtypes.bfloat16


def bf(x):
    return np.asarray(x, np.float32).astype(BF16)


def f64(x):
    return np.asarray(x).astype(np.float64)


B, C, P, NH, G, HH, WW = 4, 128, 512, 32, 16, 64, 64
N = HH * WW
EPS = 1e-5


def group_norm(x, gamma, beta):
    xg = x.reshape(B, G, (C // G) * N)
    mean = xg.mean(axis=-1, keepdims=True)
    var = xg.var(axis=-1, keepdims=True)
    xn = ((xg - mean) / np.sqrt(var + EPS)).reshape(B, C, N)
    return xn * gamma[None, :, None] + beta[None, :, None]


def setup_inputs():
    s = mx_kscale(P)
    return {
        "feat": bf(np.random.standard_normal((B, C, HH, WW))),
        "h_attn": bf(np.random.standard_normal((B, P, HH, WW)) * 0.5 * s[None, :, None, None]),
        "w_out": bf(np.random.standard_normal((C, P)) * 2.0 / np.sqrt(P) / s[None, :]),
        "b_out": bf(np.random.standard_normal(C) * 0.3),
        "gamma": bf(1.0 + 0.1 * np.random.standard_normal(C)),
        "beta": bf(0.1 * np.random.standard_normal(C)),
    }


def reference(feat, h_attn, w_out, b_out, gamma, beta):
    y = (mxq(f64(w_out), 1, "e4m3") @ mxq(f64(h_attn).reshape(B, P, N), 1, "e4m3")) + f64(b_out)[None, :, None]
    x = f64(feat).reshape(B, C, N) + y
    return group_norm(x, f64(gamma), f64(beta)).reshape(B, C, HH, WW)

@@ -1,0 +1,288 @@
+from contextlib import ExitStack
+
+import concourse.mybir as mybir
+from concourse.masks import make_identity
+
+F32 = mybir.dt.float32
+BF16 = mybir.dt.bfloat16
+U32 = mybir.dt.uint32
+U8 = mybir.dt.uint8
+FP8X4 = mybir.dt.float8_e4m3fn_x4
+ALU = mybir.AluOpType
+ACT = mybir.ActivationFunctionType
+AXIS = mybir.AxisListType
+
+P = 128
+PACK = 4
+SAMPLES = 4
+CHANNELS = 128
+K = P * PACK
+POSITIONS = 64 * 64
+GROUP = 8
+GROUPS = CHANNELS // GROUP
+EPS = 1e-5
+
+PASS_COLS = 512
+CHUNK = 1024
+HALF = POSITIONS // 2
+CHUNKS_PER_SAMPLE = POSITIONS // CHUNK
+CHUNKS = SAMPLES * CHUNKS_PER_SAMPLE
+PASSES_PER_CHUNK = CHUNK // PASS_COLS
+RAW_HALVES = 6
+
+REGROUP_VECTOR_COLS = 512
+NORM_VECTOR_COLS = 2560
+NORM_PIECES = 2
+
+FLOPS = 2 * SAMPLES * CHANNELS * K * POSITIONS
+
+
+def tile_crossattention_pa_t_kernel(tc, feat, h_attn, w_out, b_out, gamma, beta, out):
+    nc = tc.nc
+    h_rows = h_attn.rearrange("b (p j) h w -> b p j (h w)", j=PACK)
+    feat_rows = feat.rearrange("b c h w -> b c (h w)")
+    out_rows = out.rearrange("b c h w -> b c (h w)")
+
+    with ExitStack() as stack:
+        stack.enter_context(tc.manual_schedule())
+        const = stack.enter_context(tc.tile_pool(name="const", bufs=1))
+        raw_pool = stack.enter_context(tc.tile_pool(name="raw", bufs=RAW_HALVES))
+        feat_pool = stack.enter_context(tc.tile_pool(name="feat", bufs=SAMPLES))
+        grouped_pool = stack.enter_context(tc.tile_pool(name="grouped", bufs=3))
+        mx_pool = stack.enter_context(tc.tile_pool(name="mx", bufs=3))
+        x_pool = stack.enter_context(tc.tile_pool(name="x", bufs=3))
+        unread_pool = stack.enter_context(tc.tile_pool(name="unread", bufs=2))
+        stat_pool = stack.enter_context(tc.tile_pool(name="stat", bufs=2))
+        setup_psum = stack.enter_context(tc.psum_pool(name="setup_psum", bufs=1))
+        moment_psum = stack.enter_context(tc.psum_pool(name="moment_psum", bufs=2))
+        acc_psum = stack.enter_context(tc.psum_pool(name="acc_psum", bufs=2 * PASSES_PER_CHUNK))
+
+        raw = {}
+        feat_sb = {}
+        grouped = {}
+        codes = {}
+        scales = {}
+        acc = {}
+        x = {}
+        sums = {}
+        square_sums = {}
+        moments = {}
+        minus_var = {}
+        minus_mean = {}
+        std = {}
+
+        def load_h(b, first, width):
+            half, offset = divmod(first, HALF)
+            if offset == 0:
+                raw[(b, half)] = raw_pool.tile([P, PACK, HALF], BF16, name="raw")
+            nc.sync.dma_start(
+                out=raw[(b, half)][:, :, offset : offset + width],
+                in_=h_rows[b, :, :, first : first + width],
+            )
+
+        def load_feat(b):
+            feat_sb[b] = feat_pool.tile([P, POSITIONS], BF16, name="feat_sb")
+            nc.sync.dma_start(out=feat_sb[b][:], in_=feat_rows[b])
+
+        def regroup(c):
+            b, q = divmod(c, CHUNKS_PER_SAMPLE)
+            half, offset = divmod(q * CHUNK, HALF)
+            planes = raw[(b, half)][:, :, offset : offset + CHUNK]
+            grouped[c] = grouped_pool.tile([P, CHUNK, PACK], BF16, name="grouped", align_bytes=64)
+            shares = (
+                (nc.vector.tensor_copy, slice(0, REGROUP_VECTOR_COLS)),
+                (nc.scalar.copy, slice(REGROUP_VECTOR_COLS, CHUNK)),
+            )
+            for engine_copy, cols in shares:
+                engine_copy(
+                    out=grouped[c][:, cols, :].rearrange("p (w i) j -> p w j i", i=4),
+                    in_=planes[:, :, cols].rearrange("p j (w i) -> p w j i", i=4),
+                )
+
+        def quantise(c):
+            codes[c] = mx_pool.tile([P, CHUNK], U32, name="codes", align_bytes=64)
+            scales[c] = mx_pool.tile([P, CHUNK], U8, name="scales", align_bytes=64)
+            nc.vector.quantize_mx(
+                out=codes[c][:].bitcast(FP8X4),
+                scales=scales[c][:],
+                in_=grouped[c][:].rearrange("p w j -> p (w j)"),
+            )
+
+        def multiply(c):
+            for s in range(PASSES_PER_CHUNK):
+                cols = slice(s * PASS_COLS, (s + 1) * PASS_COLS)
+                acc[(c, s)] = acc_psum.tile([P, PASS_COLS], F32, name="acc")
+                nc.tensor.matmul_mx(
+                    out=acc[(c, s)][:],
+                    lhsT=w_codes[:].bitcast(FP8X4),
+                    lhsT_scale=w_scales[:],
+                    rhs=codes[c][:, cols].bitcast(FP8X4),
+                    rhs_scale=scales[c][:, cols],
+                    start=True,
+                    stop=True,
+                )
+
+        def residual(c):
+            b, q = divmod(c, CHUNKS_PER_SAMPLE)
+            if q == 0:
+                x[b] = x_pool.tile([P, POSITIONS], F32, name="x")
+                sums[b] = stat_pool.tile([P, POSITIONS // PASS_COLS], F32, name="sums")
+                square_sums[b] = stat_pool.tile([P, CHUNKS_PER_SAMPLE], F32, name="square_sums")
+            for s in range(PASSES_PER_CHUNK):
+                bank = q * PASSES_PER_CHUNK + s
+                cols = slice(bank * PASS_COLS, (bank + 1) * PASS_COLS)
+                nc.vector.scalar_tensor_tensor(
+                    out=x[b][:, cols],
+                    in0=acc[(c, s)][:],
+                    scalar=bias_col,
+                    in1=feat_sb[b][:, cols],
+                    op0=ALU.add,
+                    op1=ALU.add,
+                    accum_out=sums[b][:, bank : bank + 1],
+                )
+
+        def squares(c):
+            b, q = divmod(c, CHUNKS_PER_SAMPLE)
+            unread = unread_pool.tile([P, CHUNK], BF16, name="unread")
+            nc.scalar.activation(
+                out=unread[:],
+                in_=x[b][:, q * CHUNK : (q + 1) * CHUNK],
+                func=ACT.Square,
+                accum_out=square_sums[b][:, q : q + 1],
+            )
+
+        def group_moments(b):
+            totals = stat_pool.tile([P, 2], F32, name="totals")
+            nc.vector.tensor_reduce(out=totals[:, 0:1], in_=sums[b][:], axis=AXIS.X, op=ALU.add)
+            nc.vector.tensor_reduce(out=totals[:, 1:2], in_=square_sums[b][:], axis=AXIS.X, op=ALU.add)
+            moments_ps = moment_psum.tile([P, 2], F32, name="moments_ps")
+            nc.tensor.matmul(out=moments_ps[:], lhsT=averager_2d, rhs=totals[:], start=True, stop=True)
+            moments[b] = moments_ps
+
+        def deviation(b):
+            both = stat_pool.tile([P, 2], F32, name="both")
+            nc.vector.tensor_copy(out=both[:], in_=moments[b][:])
+            minus_var[b] = stat_pool.tile([P, 1], F32, name="minus_var")
+            nc.vector.scalar_tensor_tensor(
+                out=minus_var[b][:],
+                in0=both[:, 0:1],
+                scalar=both[:, 0:1],
+                in1=both[:, 1:2],
+                op0=ALU.mult,
+                op1=ALU.subtract,
+            )
+            std[b] = stat_pool.tile([P, 1], F32, name="std")
+            nc.scalar.activation(out=std[b][:], in_=minus_var[b][:], func=ACT.Sqrt, scale=-1.0, bias=eps_col[:])
+            minus_mean[b] = stat_pool.tile([P, 1], F32, name="minus_mean")
+            nc.vector.tensor_scalar(
+                out=minus_mean[b][:], in0=both[:, 0:1], scalar1=-1.0, scalar2=None, op0=ALU.mult
+            )
+
+        def normalise(b):
+            gain = stat_pool.tile([P, 1], F32, name="gain")
+            shift = stat_pool.tile([P, 1], F32, name="shift")
+            nc.vector.reciprocal(out=gain[:], in_=std[b][:])
+            nc.vector.tensor_mul(out=gain[:], in0=gain[:], in1=gamma_col)
+            nc.vector.scalar_tensor_tensor(
+                out=shift[:], in0=gain[:], scalar=minus_mean[b][:], in1=beta_col, op0=ALU.mult, op1=ALU.add
+            )
+            vector_cols = NORM_VECTOR_COLS // NORM_PIECES
+            scalar_cols = (POSITIONS - NORM_VECTOR_COLS) // NORM_PIECES
+            for piece in range(NORM_PIECES):
+                cols = slice(piece * vector_cols, (piece + 1) * vector_cols)
+                nc.vector.tensor_scalar(
+                    out=x[b][:, cols], in0=x[b][:, cols], scalar1=gain[:], scalar2=shift[:], op0=ALU.mult, op1=ALU.add
+                )
+                nc.sync.dma_start(out=out_rows[b, :, cols], in_=x[b][:, cols])
+                first = NORM_VECTOR_COLS + piece * scalar_cols
+                cols = slice(first, first + scalar_cols)
+                nc.scalar.activation(
+                    out=x[b][:, cols], in_=x[b][:, cols], func=ACT.Identity, scale=gain[:], bias=shift[:]
+                )
+                nc.sync.dma_start(out=out_rows[b, :, cols], in_=x[b][:, cols])
+
+        w_sb = const.tile([P, K], BF16, name="w_sb")
+        nc.scalar.dma_start(out=w_sb[:], in_=w_out)
+        vector_rows = const.tile([P, P], BF16, name="vector_rows")
+        nc.vector.memset(vector_rows[:], 0.0)
+        for row, vector in enumerate((b_out, gamma, beta)):
+            nc.scalar.dma_start(out=vector_rows[row : row + 1, :], in_=vector.rearrange("(o c) -> o c", o=1))
+
+        load_h(0, 0, REGROUP_VECTOR_COLS)
+        load_h(0, REGROUP_VECTOR_COLS, CHUNK - REGROUP_VECTOR_COLS)
+        load_h(0, CHUNK, CHUNK)
+        load_h(0, 2 * CHUNK, CHUNK)
+        load_feat(0)
+        load_h(0, 3 * CHUNK, CHUNK)
+        for b in range(1, RAW_HALVES // 2):
+            load_h(b, 0, HALF)
+            load_feat(b)
+            load_h(b, HALF, HALF)
+
+        eps_col = const.tile([P, 1], F32, name="eps_col")
+        nc.vector.memset(eps_col[:], EPS)
+        table_warmer = const.tile([P, 1], F32, name="table_warmer")
+        nc.scalar.activation(out=table_warmer[:], in_=eps_col[:], func=ACT.Sqrt)
+        identity = const.tile([P, P], F32, name="identity")
+        make_identity(nc, identity[:])
+        member = const.tile([P, GROUPS], F32, name="member")
+        nc.vector.tensor_reduce(
+            out=member[:], in_=identity[:].rearrange("k (g i) -> k g i", i=GROUP), axis=AXIS.X, op=ALU.add
+        )
+        averager = const.tile([P, GROUPS, GROUP], F32, name="averager")
+        nc.vector.tensor_scalar(
+            out=averager[:],
+            in0=member[:].unsqueeze(2).to_broadcast([P, GROUPS, GROUP]),
+            scalar1=1.0 / (GROUP * POSITIONS),
+            scalar2=None,
+            op0=ALU.mult,
+        )
+        averager_2d = averager[:].rearrange("k g i -> k (g i)")
+
+        regroup(0)
+
+        w_words = w_sb[:].bitcast(F32).rearrange("o (p u) -> o u p", u=2)
+        w_turned = setup_psum.tile([P, 2, CHANNELS], F32, name="w_turned")
+        for u in range(2):
+            nc.tensor.transpose(w_turned[:, u, :], w_words[:, u, :], identity[:])
+        w_grouped = const.tile([P, CHANNELS * PACK], BF16, name="w_grouped", align_bytes=64)
+        nc.vector.tensor_copy(
+            out=w_grouped[:].bitcast(F32).rearrange("p (o u) -> p o u", u=2),
+            in_=w_turned[:].rearrange("p u o -> p o u"),
+        )
+        w_codes = const.tile([P, CHANNELS], U32, name="w_codes", align_bytes=64)
+        w_scales = const.tile([P, CHANNELS], U8, name="w_scales", align_bytes=64)
+        nc.vector.quantize_mx(out=w_codes[:].bitcast(FP8X4), scales=w_scales[:], in_=w_grouped[:])
+
+        vector_rows_f32 = const.tile([P, P], F32, name="vector_rows_f32")
+        nc.vector.tensor_copy(out=vector_rows_f32[:], in_=vector_rows[:])
+        vector_cols_ps = setup_psum.tile([P, P], F32, name="vector_cols_ps")
+        nc.tensor.transpose(vector_cols_ps[:], vector_rows_f32[:], identity[:])
+        vector_cols = const.tile([P, 3], F32, name="vector_cols")
+        nc.vector.tensor_copy(out=vector_cols[:], in_=vector_cols_ps[:, 0:3])
+        bias_col = vector_cols[:, 0:1]
+        gamma_col = vector_cols[:, 1:2]
+        beta_col = vector_cols[:, 2:3]
+
+        for t in range(1, CHUNKS + 3):
+            done, rest = divmod(t - 3, CHUNKS_PER_SAMPLE)
+            finished = done if (t >= 3 and rest == CHUNKS_PER_SAMPLE - 1) else None
+            if t % 2 == 0 and t // 2 - 1 + RAW_HALVES < 2 * SAMPLES:
+                b, half = divmod(t // 2 - 1 + RAW_HALVES, 2)
+                load_h(b, half * HALF, HALF)
+                if half == 0:
+                    load_feat(b)
+            if t < CHUNKS:
+                regroup(t)
+            if finished is not None:
+                group_moments(finished)
+            if t - 1 < CHUNKS:
+                quantise(t - 1)
+                multiply(t - 1)
+            if finished is not None:
+                deviation(finished)
+            if 0 <= t - 2 < CHUNKS:
+                residual(t - 2)
+                squares(t - 2)
+            if finished is not None:
+                normalise(finished)

@@ -28,9 +28,9 @@ HALF = POSITIONS // 2
 CHUNKS_PER_SAMPLE = POSITIONS // CHUNK
 CHUNKS = SAMPLES * CHUNKS_PER_SAMPLE
 PASSES_PER_CHUNK = CHUNK // PASS_COLS
-RAW_HALVES = 6
+RAW_HALVES = 5
 
-REGROUP_VECTOR_COLS = 512
+REGROUP_VECTOR_COLS = 448
 NORM_VECTOR_COLS = 2560
 NORM_PIECES = 2
 
@@ -50,10 +50,9 @@ def tile_crossattention_pa_t_kernel(tc, feat, h_attn, w_out, b_out, gamma, beta,
         feat_pool = stack.enter_context(tc.tile_pool(name="feat", bufs=SAMPLES))
         grouped_pool = stack.enter_context(tc.tile_pool(name="grouped", bufs=3))
         mx_pool = stack.enter_context(tc.tile_pool(name="mx", bufs=3))
-        x_pool = stack.enter_context(tc.tile_pool(name="x", bufs=3))
+        x_pool = stack.enter_context(tc.tile_pool(name="x", bufs=SAMPLES))
         unread_pool = stack.enter_context(tc.tile_pool(name="unread", bufs=2))
         stat_pool = stack.enter_context(tc.tile_pool(name="stat", bufs=2))
-        setup_psum = stack.enter_context(tc.psum_pool(name="setup_psum", bufs=1))
         moment_psum = stack.enter_context(tc.psum_pool(name="moment_psum", bufs=2))
         acc_psum = stack.enter_context(tc.psum_pool(name="acc_psum", bufs=2 * PASSES_PER_CHUNK))
 
@@ -66,10 +65,10 @@ def tile_crossattention_pa_t_kernel(tc, feat, h_attn, w_out, b_out, gamma, beta,
         x = {}
         sums = {}
         square_sums = {}
-        moments = {}
-        minus_var = {}
+        mean_ps = {}
+        mean_square_ps = {}
         minus_mean = {}
-        std = {}
+        inverse_std = {}
 
         def load_h(b, first, width):
             half, offset = divmod(first, HALF)
@@ -140,6 +139,11 @@ def tile_crossattention_pa_t_kernel(tc, feat, h_attn, w_out, b_out, gamma, beta,
                     op1=ALU.add,
                     accum_out=sums[b][:, bank : bank + 1],
                 )
+            if q == CHUNKS_PER_SAMPLE - 1:
+                total = stat_pool.tile([P, 1], F32, name="total")
+                nc.vector.tensor_reduce(out=total[:], in_=sums[b][:], axis=AXIS.X, op=ALU.add)
+                mean_ps[b] = moment_psum.tile([P, 1], F32, name="mean_ps")
+                nc.tensor.matmul(out=mean_ps[b][:], lhsT=averager_2d, rhs=total[:], start=True, stop=True)
 
         def squares(c):
             b, q = divmod(c, CHUNKS_PER_SAMPLE)
@@ -150,42 +154,50 @@ def tile_crossattention_pa_t_kernel(tc, feat, h_attn, w_out, b_out, gamma, beta,
                 func=ACT.Square,
                 accum_out=square_sums[b][:, q : q + 1],
             )
-
-        def group_moments(b):
-            totals = stat_pool.tile([P, 2], F32, name="totals")
-            nc.vector.tensor_reduce(out=totals[:, 0:1], in_=sums[b][:], axis=AXIS.X, op=ALU.add)
-            nc.vector.tensor_reduce(out=totals[:, 1:2], in_=square_sums[b][:], axis=AXIS.X, op=ALU.add)
-            moments_ps = moment_psum.tile([P, 2], F32, name="moments_ps")
-            nc.tensor.matmul(out=moments_ps[:], lhsT=averager_2d, rhs=totals[:], start=True, stop=True)
-            moments[b] = moments_ps
+            if q == 0:
+                mean_square_ps[b] = moment_psum.tile([P, 1], F32, name="mean_square_ps")
+            nc.tensor.matmul(
+                out=mean_square_ps[b][:],
+                lhsT=averager_2d,
+                rhs=square_sums[b][:, q : q + 1],
+                start=(q == 0),
+                stop=(q == CHUNKS_PER_SAMPLE - 1),
+            )
 
         def deviation(b):
-            both = stat_pool.tile([P, 2], F32, name="both")
-            nc.vector.tensor_copy(out=both[:], in_=moments[b][:])
-            minus_var[b] = stat_pool.tile([P, 1], F32, name="minus_var")
-            nc.vector.scalar_tensor_tensor(
-                out=minus_var[b][:],
-                in0=both[:, 0:1],
-                scalar=both[:, 0:1],
-                in1=both[:, 1:2],
-                op0=ALU.mult,
-                op1=ALU.subtract,
-            )
-            std[b] = stat_pool.tile([P, 1], F32, name="std")
-            nc.scalar.activation(out=std[b][:], in_=minus_var[b][:], func=ACT.Sqrt, scale=-1.0, bias=eps_col[:])
             minus_mean[b] = stat_pool.tile([P, 1], F32, name="minus_mean")
             nc.vector.tensor_scalar(
-                out=minus_mean[b][:], in0=both[:, 0:1], scalar1=-1.0, scalar2=None, op0=ALU.mult
+                out=minus_mean[b][:], in0=mean_ps[b][:], scalar1=-1.0, scalar2=None, op0=ALU.mult
+            )
+            shifted_eps = stat_pool.tile([P, 1], F32, name="shifted_eps")
+            nc.vector.scalar_tensor_tensor(
+                out=shifted_eps[:],
+                in0=mean_ps[b][:],
+                scalar=minus_mean[b][:],
+                in1=eps_col[:],
+                op0=ALU.mult,
+                op1=ALU.add,
+            )
+            inverse_std[b] = stat_pool.tile([P, 1], F32, name="inverse_std")
+            nc.scalar.activation(
+                out=inverse_std[b][:], in_=mean_square_ps[b][:], func=ACT.Abs_reciprocal_sqrt, bias=shifted_eps[:]
             )
 
         def normalise(b):
             gain = stat_pool.tile([P, 1], F32, name="gain")
             shift = stat_pool.tile([P, 1], F32, name="shift")
-            nc.vector.reciprocal(out=gain[:], in_=std[b][:])
-            nc.vector.tensor_mul(out=gain[:], in0=gain[:], in1=gamma_col)
+            nc.vector.tensor_mul(out=gain[:], in0=inverse_std[b][:], in1=gamma_col)
             nc.vector.scalar_tensor_tensor(
                 out=shift[:], in0=gain[:], scalar=minus_mean[b][:], in1=beta_col, op0=ALU.mult, op1=ALU.add
             )
+            if b < SAMPLES - 1:
+                for q in range(CHUNKS_PER_SAMPLE):
+                    cols = slice(q * CHUNK, (q + 1) * CHUNK)
+                    nc.gpsimd.tensor_scalar(
+                        out=x[b][:, cols], in0=x[b][:, cols], scalar1=gain[:], scalar2=shift[:], op0=ALU.mult, op1=ALU.add
+                    )
+                    nc.sync.dma_start(out=out_rows[b, :, cols], in_=x[b][:, cols])
+                return
             vector_cols = NORM_VECTOR_COLS // NORM_PIECES
             scalar_cols = (POSITIONS - NORM_VECTOR_COLS) // NORM_PIECES
             for piece in range(NORM_PIECES):
@@ -201,6 +213,12 @@ def tile_crossattention_pa_t_kernel(tc, feat, h_attn, w_out, b_out, gamma, beta,
                 )
                 nc.sync.dma_start(out=out_rows[b, :, cols], in_=x[b][:, cols])
 
+        def load_half(index):
+            b, half = divmod(index, 2)
+            load_h(b, half * HALF, HALF)
+            if half == 0:
+                load_feat(b)
+
         w_sb = const.tile([P, K], BF16, name="w_sb")
         nc.scalar.dma_start(out=w_sb[:], in_=w_out)
         vector_rows = const.tile([P, P], BF16, name="vector_rows")
@@ -214,15 +232,13 @@ def tile_crossattention_pa_t_kernel(tc, feat, h_attn, w_out, b_out, gamma, beta,
         load_h(0, 2 * CHUNK, CHUNK)
         load_feat(0)
         load_h(0, 3 * CHUNK, CHUNK)
-        for b in range(1, RAW_HALVES // 2):
-            load_h(b, 0, HALF)
-            load_feat(b)
-            load_h(b, HALF, HALF)
+        for index in range(2, RAW_HALVES):
+            load_half(index)
 
         eps_col = const.tile([P, 1], F32, name="eps_col")
         nc.vector.memset(eps_col[:], EPS)
         table_warmer = const.tile([P, 1], F32, name="table_warmer")
-        nc.scalar.activation(out=table_warmer[:], in_=eps_col[:], func=ACT.Sqrt)
+        nc.scalar.activation(out=table_warmer[:], in_=eps_col[:], func=ACT.Abs_reciprocal_sqrt)
         identity = const.tile([P, P], F32, name="identity")
         make_identity(nc, identity[:])
         member = const.tile([P, GROUPS], F32, name="member")
@@ -242,7 +258,7 @@ def tile_crossattention_pa_t_kernel(tc, feat, h_attn, w_out, b_out, gamma, beta,
         regroup(0)
 
         w_words = w_sb[:].bitcast(F32).rearrange("o (p u) -> o u p", u=2)
-        w_turned = setup_psum.tile([P, 2, CHANNELS], F32, name="w_turned")
+        w_turned = acc_psum.tile([P, 2, CHANNELS], F32, name="w_turned", tag="acc")
         for u in range(2):
             nc.tensor.transpose(w_turned[:, u, :], w_words[:, u, :], identity[:])
         w_grouped = const.tile([P, CHANNELS * PACK], BF16, name="w_grouped", align_bytes=64)
@@ -256,7 +272,7 @@ def tile_crossattention_pa_t_kernel(tc, feat, h_attn, w_out, b_out, gamma, beta,
 
         vector_rows_f32 = const.tile([P, P], F32, name="vector_rows_f32")
         nc.vector.tensor_copy(out=vector_rows_f32[:], in_=vector_rows[:])
-        vector_cols_ps = setup_psum.tile([P, P], F32, name="vector_cols_ps")
+        vector_cols_ps = acc_psum.tile([P, P], F32, name="vector_cols_ps", tag="acc")
         nc.tensor.transpose(vector_cols_ps[:], vector_rows_f32[:], identity[:])
         vector_cols = const.tile([P, 3], F32, name="vector_cols")
         nc.vector.tensor_copy(out=vector_cols[:], in_=vector_cols_ps[:, 0:3])
@@ -264,25 +280,18 @@ def tile_crossattention_pa_t_kernel(tc, feat, h_attn, w_out, b_out, gamma, beta,
         gamma_col = vector_cols[:, 1:2]
         beta_col = vector_cols[:, 2:3]
 
-        for t in range(1, CHUNKS + 3):
-            done, rest = divmod(t - 3, CHUNKS_PER_SAMPLE)
-            finished = done if (t >= 3 and rest == CHUNKS_PER_SAMPLE - 1) else None
+        for t in range(1, CHUNKS + 4):
             if t % 2 == 0 and t // 2 - 1 + RAW_HALVES < 2 * SAMPLES:
-                b, half = divmod(t // 2 - 1 + RAW_HALVES, 2)
-                load_h(b, half * HALF, HALF)
-                if half == 0:
-                    load_feat(b)
+                load_half(t // 2 - 1 + RAW_HALVES)
             if t < CHUNKS:
                 regroup(t)
-            if finished is not None:
-                group_moments(finished)
+            if t >= 3 and (t - 3) % CHUNKS_PER_SAMPLE == CHUNKS_PER_SAMPLE - 1:
+                deviation((t - 3) // CHUNKS_PER_SAMPLE)
+            if t >= 4 and (t - 4) % CHUNKS_PER_SAMPLE == CHUNKS_PER_SAMPLE - 1:
+                normalise((t - 4) // CHUNKS_PER_SAMPLE)
             if t - 1 < CHUNKS:
                 quantise(t - 1)
                 multiply(t - 1)
-            if finished is not None:
-                deviation(finished)
             if 0 <= t - 2 < CHUNKS:
                 residual(t - 2)
                 squares(t - 2)
-            if finished is not None:
-                normalise(finished)

@@ -53,6 +53,7 @@ def tile_crossattention_pa_t_kernel(tc, feat, h_attn, w_out, b_out, gamma, beta,
         x_pool = stack.enter_context(tc.tile_pool(name="x", bufs=SAMPLES))
         unread_pool = stack.enter_context(tc.tile_pool(name="unread", bufs=2))
         stat_pool = stack.enter_context(tc.tile_pool(name="stat", bufs=2))
+        handed_pool = stack.enter_context(tc.tile_pool(name="handed", bufs=CHUNKS_PER_SAMPLE))
         moment_psum = stack.enter_context(tc.psum_pool(name="moment_psum", bufs=2))
         acc_psum = stack.enter_context(tc.psum_pool(name="acc_psum", bufs=2 * PASSES_PER_CHUNK))
 
@@ -69,6 +70,7 @@ def tile_crossattention_pa_t_kernel(tc, feat, h_attn, w_out, b_out, gamma, beta,
         mean_square_ps = {}
         minus_mean = {}
         inverse_std = {}
+        gain_shift = {}
 
         def load_h(b, first, width):
             half, offset = divmod(first, HALF)
@@ -183,33 +185,47 @@ def tile_crossattention_pa_t_kernel(tc, feat, h_attn, w_out, b_out, gamma, beta,
                 out=inverse_std[b][:], in_=mean_square_ps[b][:], func=ACT.Abs_reciprocal_sqrt, bias=shifted_eps[:]
             )
 
-        def normalise(b):
-            gain = stat_pool.tile([P, 1], F32, name="gain")
-            shift = stat_pool.tile([P, 1], F32, name="shift")
-            nc.vector.tensor_mul(out=gain[:], in0=inverse_std[b][:], in1=gamma_col)
+        def factors(b):
+            gain_shift[b] = stat_pool.tile([P, 2], F32, name="gain_shift")
+            nc.vector.tensor_mul(out=gain_shift[b][:, 0:1], in0=inverse_std[b][:], in1=gamma_col)
             nc.vector.scalar_tensor_tensor(
-                out=shift[:], in0=gain[:], scalar=minus_mean[b][:], in1=beta_col, op0=ALU.mult, op1=ALU.add
+                out=gain_shift[b][:, 1:2],
+                in0=gain_shift[b][:, 0:1],
+                scalar=minus_mean[b][:],
+                in1=beta_col,
+                op0=ALU.mult,
+                op1=ALU.add,
             )
-            if b < SAMPLES - 1:
-                for q in range(CHUNKS_PER_SAMPLE):
-                    cols = slice(q * CHUNK, (q + 1) * CHUNK)
-                    nc.gpsimd.tensor_scalar(
-                        out=x[b][:, cols], in0=x[b][:, cols], scalar1=gain[:], scalar2=shift[:], op0=ALU.mult, op1=ALU.add
-                    )
-                    nc.sync.dma_start(out=out_rows[b, :, cols], in_=x[b][:, cols])
-                return
+
+        def normalise_on_gpsimd(b, q):
+            handed = handed_pool.tile([P, 2], F32, name="handed")
+            nc.vector.tensor_copy(out=handed[:], in_=gain_shift[b][:])
+            cols = slice(q * CHUNK, (q + 1) * CHUNK)
+            nc.gpsimd.tensor_scalar(
+                out=x[b][:, cols],
+                in0=x[b][:, cols],
+                scalar1=handed[:, 0:1],
+                scalar2=handed[:, 1:2],
+                op0=ALU.mult,
+                op1=ALU.add,
+            )
+            nc.sync.dma_start(out=out_rows[b, :, cols], in_=x[b][:, cols])
+
+        def normalise_last(b):
+            gain = gain_shift[b][:, 0:1]
+            shift = gain_shift[b][:, 1:2]
             vector_cols = NORM_VECTOR_COLS // NORM_PIECES
             scalar_cols = (POSITIONS - NORM_VECTOR_COLS) // NORM_PIECES
             for piece in range(NORM_PIECES):
                 cols = slice(piece * vector_cols, (piece + 1) * vector_cols)
                 nc.vector.tensor_scalar(
-                    out=x[b][:, cols], in0=x[b][:, cols], scalar1=gain[:], scalar2=shift[:], op0=ALU.mult, op1=ALU.add
+                    out=x[b][:, cols], in0=x[b][:, cols], scalar1=gain, scalar2=shift, op0=ALU.mult, op1=ALU.add
                 )
                 nc.sync.dma_start(out=out_rows[b, :, cols], in_=x[b][:, cols])
                 first = NORM_VECTOR_COLS + piece * scalar_cols
                 cols = slice(first, first + scalar_cols)
                 nc.scalar.activation(
-                    out=x[b][:, cols], in_=x[b][:, cols], func=ACT.Identity, scale=gain[:], bias=shift[:]
+                    out=x[b][:, cols], in_=x[b][:, cols], func=ACT.Identity, scale=gain, bias=shift
                 )
                 nc.sync.dma_start(out=out_rows[b, :, cols], in_=x[b][:, cols])
 
@@ -288,10 +304,14 @@ def tile_crossattention_pa_t_kernel(tc, feat, h_attn, w_out, b_out, gamma, beta,
             if t >= 3 and (t - 3) % CHUNKS_PER_SAMPLE == CHUNKS_PER_SAMPLE - 1:
                 deviation((t - 3) // CHUNKS_PER_SAMPLE)
             if t >= 4 and (t - 4) % CHUNKS_PER_SAMPLE == CHUNKS_PER_SAMPLE - 1:
-                normalise((t - 4) // CHUNKS_PER_SAMPLE)
+                factors((t - 4) // CHUNKS_PER_SAMPLE)
             if t - 1 < CHUNKS:
                 quantise(t - 1)
                 multiply(t - 1)
+            b, q = divmod(t - 3 - CHUNKS_PER_SAMPLE, CHUNKS_PER_SAMPLE)
+            if 0 <= b < SAMPLES - 1:
+                normalise_on_gpsimd(b, q)
             if 0 <= t - 2 < CHUNKS:
                 residual(t - 2)
                 squares(t - 2)
+        normalise_last(SAMPLES - 1)

@@ -22,13 +22,12 @@ GROUP = 8
 GROUPS = CHANNELS // GROUP
 EPS = 1e-5
 
-PASS_COLS = 512
+BANK = 512
 CHUNK = 1024
-HALF = POSITIONS // 2
+BANKS_PER_CHUNK = CHUNK // BANK
 CHUNKS_PER_SAMPLE = POSITIONS // CHUNK
 CHUNKS = SAMPLES * CHUNKS_PER_SAMPLE
-PASSES_PER_CHUNK = CHUNK // PASS_COLS
-RAW_HALVES = 5
+RAW_CHUNKS = 10
 
 REGROUP_VECTOR_COLS = 448
 NORM_VECTOR_COLS = 2560
@@ -46,23 +45,23 @@ def tile_crossattention_pa_t_kernel(tc, feat, h_attn, w_out, b_out, gamma, beta,
     with ExitStack() as stack:
         stack.enter_context(tc.manual_schedule())
         const = stack.enter_context(tc.tile_pool(name="const", bufs=1))
-        raw_pool = stack.enter_context(tc.tile_pool(name="raw", bufs=RAW_HALVES))
+        raw_pool = stack.enter_context(tc.tile_pool(name="raw", bufs=RAW_CHUNKS))
         feat_pool = stack.enter_context(tc.tile_pool(name="feat", bufs=SAMPLES))
+        x_pool = stack.enter_context(tc.tile_pool(name="x", bufs=SAMPLES))
         grouped_pool = stack.enter_context(tc.tile_pool(name="grouped", bufs=3))
         mx_pool = stack.enter_context(tc.tile_pool(name="mx", bufs=3))
-        x_pool = stack.enter_context(tc.tile_pool(name="x", bufs=SAMPLES))
         unread_pool = stack.enter_context(tc.tile_pool(name="unread", bufs=2))
         stat_pool = stack.enter_context(tc.tile_pool(name="stat", bufs=2))
         handed_pool = stack.enter_context(tc.tile_pool(name="handed", bufs=CHUNKS_PER_SAMPLE))
         moment_psum = stack.enter_context(tc.psum_pool(name="moment_psum", bufs=2))
-        acc_psum = stack.enter_context(tc.psum_pool(name="acc_psum", bufs=2 * PASSES_PER_CHUNK))
+        y_psum = stack.enter_context(tc.psum_pool(name="y_psum", bufs=2 * BANKS_PER_CHUNK))
 
         raw = {}
-        feat_sb = {}
         grouped = {}
         codes = {}
         scales = {}
-        acc = {}
+        y = {}
+        feat_sb = {}
         x = {}
         sums = {}
         square_sums = {}
@@ -72,23 +71,20 @@ def tile_crossattention_pa_t_kernel(tc, feat, h_attn, w_out, b_out, gamma, beta,
         inverse_std = {}
         gain_shift = {}
 
-        def load_h(b, first, width):
-            half, offset = divmod(first, HALF)
-            if offset == 0:
-                raw[(b, half)] = raw_pool.tile([P, PACK, HALF], BF16, name="raw")
-            nc.sync.dma_start(
-                out=raw[(b, half)][:, :, offset : offset + width],
-                in_=h_rows[b, :, :, first : first + width],
-            )
-
-        def load_feat(b):
-            feat_sb[b] = feat_pool.tile([P, POSITIONS], BF16, name="feat_sb")
-            nc.sync.dma_start(out=feat_sb[b][:], in_=feat_rows[b])
+        def load_chunk(c):
+            b, q = divmod(c, CHUNKS_PER_SAMPLE)
+            raw[c] = raw_pool.tile([P, PACK, CHUNK], BF16, name="raw")
+            bounds = (0, REGROUP_VECTOR_COLS, CHUNK) if c == 0 else (0, CHUNK)
+            for first, end in zip(bounds, bounds[1:]):
+                nc.sync.dma_start(
+                    out=raw[c][:, :, first:end],
+                    in_=h_rows[b, :, :, q * CHUNK + first : q * CHUNK + end],
+                )
+            if q == 2:
+                feat_sb[b] = feat_pool.tile([P, POSITIONS], BF16, name="feat_sb")
+                nc.sync.dma_start(out=feat_sb[b][:], in_=feat_rows[b])
 
         def regroup(c):
-            b, q = divmod(c, CHUNKS_PER_SAMPLE)
-            half, offset = divmod(q * CHUNK, HALF)
-            planes = raw[(b, half)][:, :, offset : offset + CHUNK]
             grouped[c] = grouped_pool.tile([P, CHUNK, PACK], BF16, name="grouped", align_bytes=64)
             shares = (
                 (nc.vector.tensor_copy, slice(0, REGROUP_VECTOR_COLS)),
@@ -97,7 +93,7 @@ def tile_crossattention_pa_t_kernel(tc, feat, h_attn, w_out, b_out, gamma, beta,
             for engine_copy, cols in shares:
                 engine_copy(
                     out=grouped[c][:, cols, :].rearrange("p (w i) j -> p w j i", i=4),
-                    in_=planes[:, :, cols].rearrange("p j (w i) -> p w j i", i=4),
+                    in_=raw[c][:, :, cols].rearrange("p j (w i) -> p w j i", i=4),
                 )
 
         def quantise(c):
@@ -106,15 +102,15 @@ def tile_crossattention_pa_t_kernel(tc, feat, h_attn, w_out, b_out, gamma, beta,
             nc.vector.quantize_mx(
                 out=codes[c][:].bitcast(FP8X4),
                 scales=scales[c][:],
-                in_=grouped[c][:].rearrange("p w j -> p (w j)"),
+                in_=grouped[c][:].rearrange("p n j -> p (n j)"),
             )
 
         def multiply(c):
-            for s in range(PASSES_PER_CHUNK):
-                cols = slice(s * PASS_COLS, (s + 1) * PASS_COLS)
-                acc[(c, s)] = acc_psum.tile([P, PASS_COLS], F32, name="acc")
+            for s in range(BANKS_PER_CHUNK):
+                cols = slice(s * BANK, (s + 1) * BANK)
+                y[(c, s)] = y_psum.tile([P, BANK], F32, name="y")
                 nc.tensor.matmul_mx(
-                    out=acc[(c, s)][:],
+                    out=y[(c, s)][:],
                     lhsT=w_codes[:].bitcast(FP8X4),
                     lhsT_scale=w_scales[:],
                     rhs=codes[c][:, cols].bitcast(FP8X4),
@@ -127,14 +123,13 @@ def tile_crossattention_pa_t_kernel(tc, feat, h_attn, w_out, b_out, gamma, beta,
             b, q = divmod(c, CHUNKS_PER_SAMPLE)
             if q == 0:
                 x[b] = x_pool.tile([P, POSITIONS], F32, name="x")
-                sums[b] = stat_pool.tile([P, POSITIONS // PASS_COLS], F32, name="sums")
-                square_sums[b] = stat_pool.tile([P, CHUNKS_PER_SAMPLE], F32, name="square_sums")
-            for s in range(PASSES_PER_CHUNK):
-                bank = q * PASSES_PER_CHUNK + s
-                cols = slice(bank * PASS_COLS, (bank + 1) * PASS_COLS)
+                sums[b] = stat_pool.tile([P, POSITIONS // BANK], F32, name="sums")
+            for s in range(BANKS_PER_CHUNK):
+                bank = q * BANKS_PER_CHUNK + s
+                cols = slice(bank * BANK, (bank + 1) * BANK)
                 nc.vector.scalar_tensor_tensor(
                     out=x[b][:, cols],
-                    in0=acc[(c, s)][:],
+                    in0=y[(c, s)][:],
                     scalar=bias_col,
                     in1=feat_sb[b][:, cols],
                     op0=ALU.add,
@@ -149,6 +144,9 @@ def tile_crossattention_pa_t_kernel(tc, feat, h_attn, w_out, b_out, gamma, beta,
 
         def squares(c):
             b, q = divmod(c, CHUNKS_PER_SAMPLE)
+            if q == 0:
+                square_sums[b] = stat_pool.tile([P, CHUNKS_PER_SAMPLE], F32, name="square_sums")
+                mean_square_ps[b] = moment_psum.tile([P, 1], F32, name="mean_square_ps")
             unread = unread_pool.tile([P, CHUNK], BF16, name="unread")
             nc.scalar.activation(
                 out=unread[:],
@@ -156,8 +154,6 @@ def tile_crossattention_pa_t_kernel(tc, feat, h_attn, w_out, b_out, gamma, beta,
                 func=ACT.Square,
                 accum_out=square_sums[b][:, q : q + 1],
             )
-            if q == 0:
-                mean_square_ps[b] = moment_psum.tile([P, 1], F32, name="mean_square_ps")
             nc.tensor.matmul(
                 out=mean_square_ps[b][:],
                 lhsT=averager_2d,
@@ -171,9 +167,9 @@ def tile_crossattention_pa_t_kernel(tc, feat, h_attn, w_out, b_out, gamma, beta,
             nc.vector.tensor_scalar(
                 out=minus_mean[b][:], in0=mean_ps[b][:], scalar1=-1.0, scalar2=None, op0=ALU.mult
             )
-            shifted_eps = stat_pool.tile([P, 1], F32, name="shifted_eps")
+            eps_less_square = stat_pool.tile([P, 1], F32, name="eps_less_square")
             nc.vector.scalar_tensor_tensor(
-                out=shifted_eps[:],
+                out=eps_less_square[:],
                 in0=mean_ps[b][:],
                 scalar=minus_mean[b][:],
                 in1=eps_col[:],
@@ -182,7 +178,10 @@ def tile_crossattention_pa_t_kernel(tc, feat, h_attn, w_out, b_out, gamma, beta,
             )
             inverse_std[b] = stat_pool.tile([P, 1], F32, name="inverse_std")
             nc.scalar.activation(
-                out=inverse_std[b][:], in_=mean_square_ps[b][:], func=ACT.Abs_reciprocal_sqrt, bias=shifted_eps[:]
+                out=inverse_std[b][:],
+                in_=mean_square_ps[b][:],
+                func=ACT.Abs_reciprocal_sqrt,
+                bias=eps_less_square[:],
             )
 
         def factors(b):
@@ -214,42 +213,29 @@ def tile_crossattention_pa_t_kernel(tc, feat, h_attn, w_out, b_out, gamma, beta,
         def normalise_last(b):
             gain = gain_shift[b][:, 0:1]
             shift = gain_shift[b][:, 1:2]
-            vector_cols = NORM_VECTOR_COLS // NORM_PIECES
-            scalar_cols = (POSITIONS - NORM_VECTOR_COLS) // NORM_PIECES
+            vector_piece = NORM_VECTOR_COLS // NORM_PIECES
+            scalar_piece = (POSITIONS - NORM_VECTOR_COLS) // NORM_PIECES
             for piece in range(NORM_PIECES):
-                cols = slice(piece * vector_cols, (piece + 1) * vector_cols)
+                cols = slice(piece * vector_piece, (piece + 1) * vector_piece)
                 nc.vector.tensor_scalar(
                     out=x[b][:, cols], in0=x[b][:, cols], scalar1=gain, scalar2=shift, op0=ALU.mult, op1=ALU.add
                 )
                 nc.sync.dma_start(out=out_rows[b, :, cols], in_=x[b][:, cols])
-                first = NORM_VECTOR_COLS + piece * scalar_cols
-                cols = slice(first, first + scalar_cols)
+                first = NORM_VECTOR_COLS + piece * scalar_piece
+                cols = slice(first, first + scalar_piece)
                 nc.scalar.activation(
                     out=x[b][:, cols], in_=x[b][:, cols], func=ACT.Identity, scale=gain, bias=shift
                 )
                 nc.sync.dma_start(out=out_rows[b, :, cols], in_=x[b][:, cols])
 
-        def load_half(index):
-            b, half = divmod(index, 2)
-            load_h(b, half * HALF, HALF)
-            if half == 0:
-                load_feat(b)
-
         w_sb = const.tile([P, K], BF16, name="w_sb")
         nc.scalar.dma_start(out=w_sb[:], in_=w_out)
-        vector_rows = const.tile([P, P], BF16, name="vector_rows")
-        nc.vector.memset(vector_rows[:], 0.0)
-        for row, vector in enumerate((b_out, gamma, beta)):
-            nc.scalar.dma_start(out=vector_rows[row : row + 1, :], in_=vector.rearrange("(o c) -> o c", o=1))
-
-        load_h(0, 0, REGROUP_VECTOR_COLS)
-        load_h(0, REGROUP_VECTOR_COLS, CHUNK - REGROUP_VECTOR_COLS)
-        load_h(0, CHUNK, CHUNK)
-        load_h(0, 2 * CHUNK, CHUNK)
-        load_feat(0)
-        load_h(0, 3 * CHUNK, CHUNK)
-        for index in range(2, RAW_HALVES):
-            load_half(index)
+        param_rows = const.tile([P, P], BF16, name="param_rows")
+        nc.vector.memset(param_rows[:], 0.0)
+        for row, param in enumerate((b_out, gamma, beta)):
+            nc.scalar.dma_start(out=param_rows[row : row + 1, :], in_=param.rearrange("(o c) -> o c", o=1))
+        for c in range(RAW_CHUNKS):
+            load_chunk(c)
 
         eps_col = const.tile([P, 1], F32, name="eps_col")
         nc.vector.memset(eps_col[:], EPS)
@@ -274,7 +260,7 @@ def tile_crossattention_pa_t_kernel(tc, feat, h_attn, w_out, b_out, gamma, beta,
         regroup(0)
 
         w_words = w_sb[:].bitcast(F32).rearrange("o (p u) -> o u p", u=2)
-        w_turned = acc_psum.tile([P, 2, CHANNELS], F32, name="w_turned", tag="acc")
+        w_turned = y_psum.tile([P, 2, CHANNELS], F32, name="w_turned", tag="y")
         for u in range(2):
             nc.tensor.transpose(w_turned[:, u, :], w_words[:, u, :], identity[:])
         w_grouped = const.tile([P, CHANNELS * PACK], BF16, name="w_grouped", align_bytes=64)
@@ -286,19 +272,19 @@ def tile_crossattention_pa_t_kernel(tc, feat, h_attn, w_out, b_out, gamma, beta,
         w_scales = const.tile([P, CHANNELS], U8, name="w_scales", align_bytes=64)
         nc.vector.quantize_mx(out=w_codes[:].bitcast(FP8X4), scales=w_scales[:], in_=w_grouped[:])
 
-        vector_rows_f32 = const.tile([P, P], F32, name="vector_rows_f32")
-        nc.vector.tensor_copy(out=vector_rows_f32[:], in_=vector_rows[:])
-        vector_cols_ps = acc_psum.tile([P, P], F32, name="vector_cols_ps", tag="acc")
-        nc.tensor.transpose(vector_cols_ps[:], vector_rows_f32[:], identity[:])
-        vector_cols = const.tile([P, 3], F32, name="vector_cols")
-        nc.vector.tensor_copy(out=vector_cols[:], in_=vector_cols_ps[:, 0:3])
-        bias_col = vector_cols[:, 0:1]
-        gamma_col = vector_cols[:, 1:2]
-        beta_col = vector_cols[:, 2:3]
+        param_rows_f32 = const.tile([P, P], F32, name="param_rows_f32")
+        nc.vector.tensor_copy(out=param_rows_f32[:], in_=param_rows[:])
+        param_cols_ps = y_psum.tile([P, P], F32, name="param_cols_ps", tag="y")
+        nc.tensor.transpose(param_cols_ps[:], param_rows_f32[:], identity[:])
+        param_cols = const.tile([P, 3], F32, name="param_cols")
+        nc.vector.tensor_copy(out=param_cols[:], in_=param_cols_ps[:, 0:3])
+        bias_col = param_cols[:, 0:1]
+        gamma_col = param_cols[:, 1:2]
+        beta_col = param_cols[:, 2:3]
 
         for t in range(1, CHUNKS + 4):
-            if t % 2 == 0 and t // 2 - 1 + RAW_HALVES < 2 * SAMPLES:
-                load_half(t // 2 - 1 + RAW_HALVES)
+            if t - 1 + RAW_CHUNKS < CHUNKS:
+                load_chunk(t - 1 + RAW_CHUNKS)
             if t < CHUNKS:
                 regroup(t)
             if t >= 3 and (t - 3) % CHUNKS_PER_SAMPLE == CHUNKS_PER_SAMPLE - 1:

@@ -28,6 +28,8 @@ BANKS_PER_CHUNK = CHUNK // BANK
 CHUNKS_PER_SAMPLE = POSITIONS // CHUNK
 CHUNKS = SAMPLES * CHUNKS_PER_SAMPLE
 RAW_CHUNKS = 10
+FEAT_HALF = POSITIONS // 2
+CHUNKS_PER_FEAT_HALF = FEAT_HALF // CHUNK
 
 REGROUP_VECTOR_COLS = 448
 NORM_VECTOR_COLS = 2560
@@ -80,9 +82,19 @@ def tile_crossattention_pa_t_kernel(tc, feat, h_attn, w_out, b_out, gamma, beta,
                     out=raw[c][:, :, first:end],
                     in_=h_rows[b, :, :, q * CHUNK + first : q * CHUNK + end],
                 )
-            if q == 2:
+
+        def load_feat_half(index):
+            b, half = divmod(index, 2)
+            if half == 0:
                 feat_sb[b] = feat_pool.tile([P, POSITIONS], BF16, name="feat_sb")
-                nc.sync.dma_start(out=feat_sb[b][:], in_=feat_rows[b])
+            cols = slice(half * FEAT_HALF, (half + 1) * FEAT_HALF)
+            nc.sync.dma_start(out=feat_sb[b][:, cols], in_=feat_rows[b, :, cols])
+
+        def load(i):
+            if i < CHUNKS:
+                load_chunk(i)
+            if i >= 2 and i % CHUNKS_PER_FEAT_HALF == 0:
+                load_feat_half((i - 2) // CHUNKS_PER_FEAT_HALF)
 
         def regroup(c):
             grouped[c] = grouped_pool.tile([P, CHUNK, PACK], BF16, name="grouped", align_bytes=64)
@@ -234,8 +246,8 @@ def tile_crossattention_pa_t_kernel(tc, feat, h_attn, w_out, b_out, gamma, beta,
         nc.vector.memset(param_rows[:], 0.0)
         for row, param in enumerate((b_out, gamma, beta)):
             nc.scalar.dma_start(out=param_rows[row : row + 1, :], in_=param.rearrange("(o c) -> o c", o=1))
-        for c in range(RAW_CHUNKS):
-            load_chunk(c)
+        for i in range(RAW_CHUNKS):
+            load(i)
 
         eps_col = const.tile([P, 1], F32, name="eps_col")
         nc.vector.memset(eps_col[:], EPS)
@@ -283,8 +295,8 @@ def tile_crossattention_pa_t_kernel(tc, feat, h_attn, w_out, b_out, gamma, beta,
         beta_col = param_cols[:, 2:3]
 
         for t in range(1, CHUNKS + 4):
-            if t - 1 + RAW_CHUNKS < CHUNKS:
-                load_chunk(t - 1 + RAW_CHUNKS)
+            if t - 1 + RAW_CHUNKS <= CHUNKS:
+                load(t - 1 + RAW_CHUNKS)
             if t < CHUNKS:
                 regroup(t)
             if t >= 3 and (t - 3) % CHUNKS_PER_SAMPLE == CHUNKS_PER_SAMPLE - 1:

@@ -72,6 +72,7 @@ def tile_crossattention_pa_t_kernel(tc, feat, h_attn, w_out, b_out, gamma, beta,
         minus_mean = {}
         inverse_std = {}
         gain_shift = {}
+        handed_over = {}
 
         def load_chunk(c):
             b, q = divmod(c, CHUNKS_PER_SAMPLE)
@@ -208,9 +209,12 @@ def tile_crossattention_pa_t_kernel(tc, feat, h_attn, w_out, b_out, gamma, beta,
                 op1=ALU.add,
             )
 
+        def hand_over(b, q):
+            handed_over[(b, q)] = handed_pool.tile([P, 2], F32, name="handed")
+            nc.vector.tensor_copy(out=handed_over[(b, q)][:], in_=gain_shift[b][:])
+
         def normalise_on_gpsimd(b, q):
-            handed = handed_pool.tile([P, 2], F32, name="handed")
-            nc.vector.tensor_copy(out=handed[:], in_=gain_shift[b][:])
+            handed = handed_over[(b, q)]
             cols = slice(q * CHUNK, (q + 1) * CHUNK)
             nc.gpsimd.tensor_scalar(
                 out=x[b][:, cols],
@@ -303,10 +307,12 @@ def tile_crossattention_pa_t_kernel(tc, feat, h_attn, w_out, b_out, gamma, beta,
                 deviation((t - 3) // CHUNKS_PER_SAMPLE)
             if t >= 4 and (t - 4) % CHUNKS_PER_SAMPLE == CHUNKS_PER_SAMPLE - 1:
                 factors((t - 4) // CHUNKS_PER_SAMPLE)
+            b, q = divmod(t - 3 - CHUNKS_PER_SAMPLE, CHUNKS_PER_SAMPLE)
+            if 0 <= b < SAMPLES - 1:
+                hand_over(b, q)
             if t - 1 < CHUNKS:
                 quantise(t - 1)
                 multiply(t - 1)
-            b, q = divmod(t - 3 - CHUNKS_PER_SAMPLE, CHUNKS_PER_SAMPLE)
             if 0 <= b < SAMPLES - 1:
                 normalise_on_gpsimd(b, q)
             if 0 <= t - 2 < CHUNKS:

@@ -32,8 +32,7 @@ FEAT_HALF = POSITIONS // 2
 CHUNKS_PER_FEAT_HALF = FEAT_HALF // CHUNK
 
 REGROUP_VECTOR_COLS = 448
-NORM_VECTOR_COLS = 2560
-NORM_PIECES = 2
+LAST_PIECES = (("vector", 512), ("scalar", 512), ("vector", 1024), ("vector", 1024), ("scalar", 1024))
 
 FLOPS = 2 * SAMPLES * CHANNELS * K * POSITIONS
 
@@ -158,22 +157,26 @@ def tile_crossattention_pa_t_kernel(tc, feat, h_attn, w_out, b_out, gamma, beta,
         def squares(c):
             b, q = divmod(c, CHUNKS_PER_SAMPLE)
             if q == 0:
-                square_sums[b] = stat_pool.tile([P, CHUNKS_PER_SAMPLE], F32, name="square_sums")
+                square_sums[b] = stat_pool.tile([P, CHUNKS_PER_SAMPLE + 1], F32, name="square_sums")
                 mean_square_ps[b] = moment_psum.tile([P, 1], F32, name="mean_square_ps")
-            unread = unread_pool.tile([P, CHUNK], BF16, name="unread")
-            nc.scalar.activation(
-                out=unread[:],
-                in_=x[b][:, q * CHUNK : (q + 1) * CHUNK],
-                func=ACT.Square,
-                accum_out=square_sums[b][:, q : q + 1],
-            )
-            nc.tensor.matmul(
-                out=mean_square_ps[b][:],
-                lhsT=averager_2d,
-                rhs=square_sums[b][:, q : q + 1],
-                start=(q == 0),
-                stop=(q == CHUNKS_PER_SAMPLE - 1),
-            )
+            pieces = BANKS_PER_CHUNK if c == CHUNKS - 1 else 1
+            width = CHUNK // pieces
+            for piece in range(pieces):
+                unread = unread_pool.tile([P, width], BF16, name="unread")
+                first = q * CHUNK + piece * width
+                nc.scalar.activation(
+                    out=unread[:],
+                    in_=x[b][:, first : first + width],
+                    func=ACT.Square,
+                    accum_out=square_sums[b][:, q + piece : q + piece + 1],
+                )
+                nc.tensor.matmul(
+                    out=mean_square_ps[b][:],
+                    lhsT=averager_2d,
+                    rhs=square_sums[b][:, q + piece : q + piece + 1],
+                    start=(first == 0),
+                    stop=(first + width == POSITIONS),
+                )
 
         def deviation(b):
             minus_mean[b] = stat_pool.tile([P, 1], F32, name="minus_mean")
@@ -189,6 +192,7 @@ def tile_crossattention_pa_t_kernel(tc, feat, h_attn, w_out, b_out, gamma, beta,
                 op0=ALU.mult,
                 op1=ALU.add,
             )
+            nc.vector.tensor_mul(out=gamma_pairs[:, b, 1:2], in0=minus_mean[b][:], in1=gamma_col)
             inverse_std[b] = stat_pool.tile([P, 1], F32, name="inverse_std")
             nc.scalar.activation(
                 out=inverse_std[b][:],
@@ -199,12 +203,11 @@ def tile_crossattention_pa_t_kernel(tc, feat, h_attn, w_out, b_out, gamma, beta,
 
         def factors(b):
             gain_shift[b] = stat_pool.tile([P, 2], F32, name="gain_shift")
-            nc.vector.tensor_mul(out=gain_shift[b][:, 0:1], in0=inverse_std[b][:], in1=gamma_col)
             nc.vector.scalar_tensor_tensor(
-                out=gain_shift[b][:, 1:2],
-                in0=gain_shift[b][:, 0:1],
-                scalar=minus_mean[b][:],
-                in1=beta_col,
+                out=gain_shift[b][:],
+                in0=gamma_pairs[:, b, :],
+                scalar=inverse_std[b][:],
+                in1=zero_beta[:],
                 op0=ALU.mult,
                 op1=ALU.add,
             )
@@ -226,22 +229,33 @@ def tile_crossattention_pa_t_kernel(tc, feat, h_attn, w_out, b_out, gamma, beta,
             )
             nc.sync.dma_start(out=out_rows[b, :, cols], in_=x[b][:, cols])
 
+        def normalise_on_vector(b, q):
+            cols = slice(q * CHUNK, (q + 1) * CHUNK)
+            nc.vector.tensor_scalar(
+                out=x[b][:, cols],
+                in0=x[b][:, cols],
+                scalar1=gain_shift[b][:, 0:1],
+                scalar2=gain_shift[b][:, 1:2],
+                op0=ALU.mult,
+                op1=ALU.add,
+            )
+            nc.sync.dma_start(out=out_rows[b, :, cols], in_=x[b][:, cols])
+
         def normalise_last(b):
             gain = gain_shift[b][:, 0:1]
             shift = gain_shift[b][:, 1:2]
-            vector_piece = NORM_VECTOR_COLS // NORM_PIECES
-            scalar_piece = (POSITIONS - NORM_VECTOR_COLS) // NORM_PIECES
-            for piece in range(NORM_PIECES):
-                cols = slice(piece * vector_piece, (piece + 1) * vector_piece)
-                nc.vector.tensor_scalar(
-                    out=x[b][:, cols], in0=x[b][:, cols], scalar1=gain, scalar2=shift, op0=ALU.mult, op1=ALU.add
-                )
-                nc.sync.dma_start(out=out_rows[b, :, cols], in_=x[b][:, cols])
-                first = NORM_VECTOR_COLS + piece * scalar_piece
-                cols = slice(first, first + scalar_piece)
-                nc.scalar.activation(
-                    out=x[b][:, cols], in_=x[b][:, cols], func=ACT.Identity, scale=gain, bias=shift
-                )
+            first = 0
+            for engine, width in LAST_PIECES:
+                cols = slice(first, first + width)
+                first += width
+                if engine == "vector":
+                    nc.vector.tensor_scalar(
+                        out=x[b][:, cols], in0=x[b][:, cols], scalar1=gain, scalar2=shift, op0=ALU.mult, op1=ALU.add
+                    )
+                else:
+                    nc.scalar.activation(
+                        out=x[b][:, cols], in_=x[b][:, cols], func=ACT.Identity, scale=gain, bias=shift
+                    )
                 nc.sync.dma_start(out=out_rows[b, :, cols], in_=x[b][:, cols])
 
         w_sb = const.tile([P, K], BF16, name="w_sb")
@@ -255,6 +269,8 @@ def tile_crossattention_pa_t_kernel(tc, feat, h_attn, w_out, b_out, gamma, beta,
 
         eps_col = const.tile([P, 1], F32, name="eps_col")
         nc.vector.memset(eps_col[:], EPS)
+        zero_beta = const.tile([P, 2], F32, name="zero_beta")
+        nc.vector.memset(zero_beta[:], 0.0)
         table_warmer = const.tile([P, 1], F32, name="table_warmer")
         nc.scalar.activation(out=table_warmer[:], in_=eps_col[:], func=ACT.Abs_reciprocal_sqrt)
         identity = const.tile([P, P], F32, name="identity")
@@ -292,11 +308,15 @@ def tile_crossattention_pa_t_kernel(tc, feat, h_attn, w_out, b_out, gamma, beta,
         nc.vector.tensor_copy(out=param_rows_f32[:], in_=param_rows[:])
         param_cols_ps = y_psum.tile([P, P], F32, name="param_cols_ps", tag="y")
         nc.tensor.transpose(param_cols_ps[:], param_rows_f32[:], identity[:])
-        param_cols = const.tile([P, 3], F32, name="param_cols")
-        nc.vector.tensor_copy(out=param_cols[:], in_=param_cols_ps[:, 0:3])
+        param_cols = const.tile([P, 2], F32, name="param_cols")
+        nc.vector.tensor_copy(out=param_cols[:], in_=param_cols_ps[:, 0:2])
         bias_col = param_cols[:, 0:1]
         gamma_col = param_cols[:, 1:2]
-        beta_col = param_cols[:, 2:3]
+        nc.vector.tensor_copy(out=zero_beta[:, 1:2], in_=param_cols_ps[:, 2:3])
+        gamma_pairs = const.tile([P, SAMPLES, 2], F32, name="gamma_pairs")
+        nc.vector.tensor_copy(
+            out=gamma_pairs[:, :, 0:1], in_=param_cols_ps[:, 1:2].unsqueeze(1).to_broadcast([P, SAMPLES, 1])
+        )
 
         for t in range(1, CHUNKS + 4):
             if t - 1 + RAW_CHUNKS <= CHUNKS:
@@ -308,14 +328,17 @@ def tile_crossattention_pa_t_kernel(tc, feat, h_attn, w_out, b_out, gamma, beta,
             if t >= 4 and (t - 4) % CHUNKS_PER_SAMPLE == CHUNKS_PER_SAMPLE - 1:
                 factors((t - 4) // CHUNKS_PER_SAMPLE)
             b, q = divmod(t - 3 - CHUNKS_PER_SAMPLE, CHUNKS_PER_SAMPLE)
-            if 0 <= b < SAMPLES - 1:
+            on_gpsimd = 0 <= b < SAMPLES - 1 and t - 2 < CHUNKS
+            if on_gpsimd:
                 hand_over(b, q)
             if t - 1 < CHUNKS:
                 quantise(t - 1)
                 multiply(t - 1)
-            if 0 <= b < SAMPLES - 1:
+            if on_gpsimd:
                 normalise_on_gpsimd(b, q)
             if 0 <= t - 2 < CHUNKS:
                 residual(t - 2)
                 squares(t - 2)
+            if t - 2 == CHUNKS - 1:
+                normalise_on_vector(SAMPLES - 2, CHUNKS_PER_SAMPLE - 1)
         normalise_last(SAMPLES - 1)

@@ -32,6 +32,8 @@ FEAT_HALF = POSITIONS // 2
 CHUNKS_PER_FEAT_HALF = FEAT_HALF // CHUNK
 
 REGROUP_VECTOR_COLS = 448
+REGROUP_GPSIMD_COLS = 192
+REGROUP_VECTOR_COLS_BESIDE_GPSIMD = 328
 LAST_PIECES = (("vector", 512), ("scalar", 512), ("vector", 1024), ("vector", 1024), ("scalar", 1024))
 
 FLOPS = 2 * SAMPLES * CHANNELS * K * POSITIONS
@@ -96,11 +98,33 @@ def tile_crossattention_pa_t_kernel(tc, feat, h_attn, w_out, b_out, gamma, beta,
             if i >= 2 and i % CHUNKS_PER_FEAT_HALF == 0:
                 load_feat_half((i - 2) // CHUNKS_PER_FEAT_HALF)
 
+        def share_bounds(c):
+            if 2 <= c < 3 + CHUNKS_PER_SAMPLE:
+                return (
+                    REGROUP_VECTOR_COLS_BESIDE_GPSIMD,
+                    REGROUP_VECTOR_COLS_BESIDE_GPSIMD + REGROUP_GPSIMD_COLS,
+                )
+            return (REGROUP_VECTOR_COLS, REGROUP_VECTOR_COLS)
+
+        def regroup_on_gpsimd(c):
+            first, end = share_bounds(c)
+            glance = handed_pool.tile([P, 1, PACK], BF16, name="glance")
+            nc.gpsimd.tensor_copy(out=glance[:], in_=grouped[c][:, 0:1, :])
+            nc.gpsimd.tensor_scalar(
+                out=grouped[c][:, first:end, :],
+                in0=raw[c][:, :, first:end].rearrange("p j n -> p n j"),
+                scalar1=1.0,
+                scalar2=0.0,
+                op0=ALU.mult,
+                op1=ALU.add,
+            )
+
         def regroup(c):
             grouped[c] = grouped_pool.tile([P, CHUNK, PACK], BF16, name="grouped", align_bytes=64)
+            vector_end, scalar_first = share_bounds(c)
             shares = (
-                (nc.vector.tensor_copy, slice(0, REGROUP_VECTOR_COLS)),
-                (nc.scalar.copy, slice(REGROUP_VECTOR_COLS, CHUNK)),
+                (nc.vector.tensor_copy, slice(0, vector_end)),
+                (nc.scalar.copy, slice(scalar_first, CHUNK)),
             )
             for engine_copy, cols in shares:
                 engine_copy(
@@ -192,7 +216,9 @@ def tile_crossattention_pa_t_kernel(tc, feat, h_attn, w_out, b_out, gamma, beta,
                 op0=ALU.mult,
                 op1=ALU.add,
             )
-            nc.vector.tensor_mul(out=gamma_pairs[:, b, 1:2], in0=minus_mean[b][:], in1=gamma_col)
+            nc.vector.tensor_scalar(
+                out=gamma_pairs[:, b, 1:2], in0=mean_ps[b][:], scalar1=gamma_col, scalar2=-1.0, op0=ALU.mult, op1=ALU.mult
+            )
             inverse_std[b] = stat_pool.tile([P, 1], F32, name="inverse_std")
             nc.scalar.activation(
                 out=inverse_std[b][:],
@@ -323,8 +349,8 @@ def tile_crossattention_pa_t_kernel(tc, feat, h_attn, w_out, b_out, gamma, beta,
                 load(t - 1 + RAW_CHUNKS)
             if t < CHUNKS:
                 regroup(t)
-            if t >= 3 and (t - 3) % CHUNKS_PER_SAMPLE == CHUNKS_PER_SAMPLE - 1:
-                deviation((t - 3) // CHUNKS_PER_SAMPLE)
+                if share_bounds(t)[0] < share_bounds(t)[1]:
+                    regroup_on_gpsimd(t)
             if t >= 4 and (t - 4) % CHUNKS_PER_SAMPLE == CHUNKS_PER_SAMPLE - 1:
                 factors((t - 4) // CHUNKS_PER_SAMPLE)
             b, q = divmod(t - 3 - CHUNKS_PER_SAMPLE, CHUNKS_PER_SAMPLE)
@@ -334,6 +360,8 @@ def tile_crossattention_pa_t_kernel(tc, feat, h_attn, w_out, b_out, gamma, beta,
             if t - 1 < CHUNKS:
                 quantise(t - 1)
                 multiply(t - 1)
+            if t >= 3 and (t - 3) % CHUNKS_PER_SAMPLE == CHUNKS_PER_SAMPLE - 1:
+                deviation((t - 3) // CHUNKS_PER_SAMPLE)
             if on_gpsimd:
                 normalise_on_gpsimd(b, q)
             if 0 <= t - 2 < CHUNKS:

@@ -32,8 +32,9 @@ FEAT_HALF = POSITIONS // 2
 CHUNKS_PER_FEAT_HALF = FEAT_HALF // CHUNK
 
 REGROUP_VECTOR_COLS = 448
+RUN = 8
 REGROUP_GPSIMD_COLS = 192
-REGROUP_VECTOR_COLS_BESIDE_GPSIMD = 328
+REGROUP_VECTOR_COLS_BESIDE_GPSIMD = 320
 LAST_PIECES = (("vector", 512), ("scalar", 512), ("vector", 1024), ("vector", 1024), ("scalar", 1024))
 
 FLOPS = 2 * SAMPLES * CHANNELS * K * POSITIONS
@@ -128,8 +129,8 @@ def tile_crossattention_pa_t_kernel(tc, feat, h_attn, w_out, b_out, gamma, beta,
             )
             for engine_copy, cols in shares:
                 engine_copy(
-                    out=grouped[c][:, cols, :].rearrange("p (w i) j -> p w j i", i=4),
-                    in_=raw[c][:, :, cols].rearrange("p j (w i) -> p w j i", i=4),
+                    out=grouped[c][:, cols, :].rearrange("p (w i) j -> p w j i", i=RUN),
+                    in_=raw[c][:, :, cols].rearrange("p j (w i) -> p w j i", i=RUN),
                 )
 
         def quantise(c):

from contextlib import ExitStack

import concourse.mybir as mybir
from concourse.masks import make_identity

F32 = mybir.dt.float32
BF16 = mybir.dt.bfloat16
U32 = mybir.dt.uint32
U8 = mybir.dt.uint8
FP8X4 = mybir.dt.float8_e4m3fn_x4
ALU = mybir.AluOpType
ACT = mybir.ActivationFunctionType
AXIS = mybir.AxisListType

P = 128
PACK = 4
SAMPLES = 4
CHANNELS = 128
K = P * PACK
POSITIONS = 64 * 64
GROUP = 8
GROUPS = CHANNELS // GROUP
EPS = 1e-5

BANK = 512
CHUNK = 1024
BANKS_PER_CHUNK = CHUNK // BANK
CHUNKS_PER_SAMPLE = POSITIONS // CHUNK
CHUNKS = SAMPLES * CHUNKS_PER_SAMPLE
RAW_CHUNKS = 10
FEAT_HALF = POSITIONS // 2
CHUNKS_PER_FEAT_HALF = FEAT_HALF // CHUNK

REGROUP_VECTOR_COLS = 448
RUN = 8
REGROUP_GPSIMD_COLS = 192
REGROUP_VECTOR_COLS_BESIDE_GPSIMD = 320
LAST_PIECES = (("vector", 512), ("scalar", 512), ("vector", 1024), ("vector", 1024), ("scalar", 1024))

FLOPS = 2 * SAMPLES * CHANNELS * K * POSITIONS


def tile_crossattention_pa_t_kernel(tc, feat, h_attn, w_out, b_out, gamma, beta, out):
    nc = tc.nc
    h_rows = h_attn.rearrange("b (p j) h w -> b p j (h w)", j=PACK)
    feat_rows = feat.rearrange("b c h w -> b c (h w)")
    out_rows = out.rearrange("b c h w -> b c (h w)")

    with ExitStack() as stack:
        stack.enter_context(tc.manual_schedule())
        const = stack.enter_context(tc.tile_pool(name="const", bufs=1))
        raw_pool = stack.enter_context(tc.tile_pool(name="raw", bufs=RAW_CHUNKS))
        feat_pool = stack.enter_context(tc.tile_pool(name="feat", bufs=SAMPLES))
        x_pool = stack.enter_context(tc.tile_pool(name="x", bufs=SAMPLES))
        grouped_pool = stack.enter_context(tc.tile_pool(name="grouped", bufs=3))
        mx_pool = stack.enter_context(tc.tile_pool(name="mx", bufs=3))
        unread_pool = stack.enter_context(tc.tile_pool(name="unread", bufs=2))
        stat_pool = stack.enter_context(tc.tile_pool(name="stat", bufs=2))
        handed_pool = stack.enter_context(tc.tile_pool(name="handed", bufs=CHUNKS_PER_SAMPLE))
        moment_psum = stack.enter_context(tc.psum_pool(name="moment_psum", bufs=2))
        y_psum = stack.enter_context(tc.psum_pool(name="y_psum", bufs=2 * BANKS_PER_CHUNK))

        raw = {}
        grouped = {}
        codes = {}
        scales = {}
        y = {}
        feat_sb = {}
        x = {}
        sums = {}
        square_sums = {}
        mean_ps = {}
        mean_square_ps = {}
        minus_mean = {}
        inverse_std = {}
        gain_shift = {}
        handed_over = {}

        def load_chunk(c):
            b, q = divmod(c, CHUNKS_PER_SAMPLE)
            raw[c] = raw_pool.tile([P, PACK, CHUNK], BF16, name="raw")
            bounds = (0, REGROUP_VECTOR_COLS, CHUNK) if c == 0 else (0, CHUNK)
            for first, end in zip(bounds, bounds[1:]):
                nc.sync.dma_start(
                    out=raw[c][:, :, first:end],
                    in_=h_rows[b, :, :, q * CHUNK + first : q * CHUNK + end],
                )

        def load_feat_half(index):
            b, half = divmod(index, 2)
            if half == 0:
                feat_sb[b] = feat_pool.tile([P, POSITIONS], BF16, name="feat_sb")
            cols = slice(half * FEAT_HALF, (half + 1) * FEAT_HALF)
            nc.sync.dma_start(out=feat_sb[b][:, cols], in_=feat_rows[b, :, cols])

        def load(i):
            if i < CHUNKS:
                load_chunk(i)
            if i >= 2 and i % CHUNKS_PER_FEAT_HALF == 0:
                load_feat_half((i - 2) // CHUNKS_PER_FEAT_HALF)

        def share_bounds(c):
            if 2 <= c < 3 + CHUNKS_PER_SAMPLE:
                return (
                    REGROUP_VECTOR_COLS_BESIDE_GPSIMD,
                    REGROUP_VECTOR_COLS_BESIDE_GPSIMD + REGROUP_GPSIMD_COLS,
                )
            return (REGROUP_VECTOR_COLS, REGROUP_VECTOR_COLS)

        def regroup_on_gpsimd(c):
            first, end = share_bounds(c)
            glance = handed_pool.tile([P, 1, PACK], BF16, name="glance")
            nc.gpsimd.tensor_copy(out=glance[:], in_=grouped[c][:, 0:1, :])
            nc.gpsimd.tensor_scalar(
                out=grouped[c][:, first:end, :],
                in0=raw[c][:, :, first:end].rearrange("p j n -> p n j"),
                scalar1=1.0,
                scalar2=0.0,
                op0=ALU.mult,
                op1=ALU.add,
            )

        def regroup(c):
            grouped[c] = grouped_pool.tile([P, CHUNK, PACK], BF16, name="grouped", align_bytes=64)
            vector_end, scalar_first = share_bounds(c)
            shares = (
                (nc.vector.tensor_copy, slice(0, vector_end)),
                (nc.scalar.copy, slice(scalar_first, CHUNK)),
            )
            for engine_copy, cols in shares:
                engine_copy(
                    out=grouped[c][:, cols, :].rearrange("p (w i) j -> p w j i", i=RUN),
                    in_=raw[c][:, :, cols].rearrange("p j (w i) -> p w j i", i=RUN),
                )

        def quantise(c):
            codes[c] = mx_pool.tile([P, CHUNK], U32, name="codes", align_bytes=64)
            scales[c] = mx_pool.tile([P, CHUNK], U8, name="scales", align_bytes=64)
            nc.vector.quantize_mx(
                out=codes[c][:].bitcast(FP8X4),
                scales=scales[c][:],
                in_=grouped[c][:].rearrange("p n j -> p (n j)"),
            )

        def multiply(c):
            for s in range(BANKS_PER_CHUNK):
                cols = slice(s * BANK, (s + 1) * BANK)
                y[(c, s)] = y_psum.tile([P, BANK], F32, name="y")
                nc.tensor.matmul_mx(
                    out=y[(c, s)][:],
                    lhsT=w_codes[:].bitcast(FP8X4),
                    lhsT_scale=w_scales[:],
                    rhs=codes[c][:, cols].bitcast(FP8X4),
                    rhs_scale=scales[c][:, cols],
                    start=True,
                    stop=True,
                )

        def residual(c):
            b, q = divmod(c, CHUNKS_PER_SAMPLE)
            if q == 0:
                x[b] = x_pool.tile([P, POSITIONS], F32, name="x")
                sums[b] = stat_pool.tile([P, POSITIONS // BANK], F32, name="sums")
            for s in range(BANKS_PER_CHUNK):
                bank = q * BANKS_PER_CHUNK + s
                cols = slice(bank * BANK, (bank + 1) * BANK)
                nc.vector.scalar_tensor_tensor(
                    out=x[b][:, cols],
                    in0=y[(c, s)][:],
                    scalar=bias_col,
                    in1=feat_sb[b][:, cols],
                    op0=ALU.add,
                    op1=ALU.add,
                    accum_out=sums[b][:, bank : bank + 1],
                )
            if q == CHUNKS_PER_SAMPLE - 1:
                total = stat_pool.tile([P, 1], F32, name="total")
                nc.vector.tensor_reduce(out=total[:], in_=sums[b][:], axis=AXIS.X, op=ALU.add)
                mean_ps[b] = moment_psum.tile([P, 1], F32, name="mean_ps")
                nc.tensor.matmul(out=mean_ps[b][:], lhsT=averager_2d, rhs=total[:], start=True, stop=True)

        def squares(c):
            b, q = divmod(c, CHUNKS_PER_SAMPLE)
            if q == 0:
                square_sums[b] = stat_pool.tile([P, CHUNKS_PER_SAMPLE + 1], F32, name="square_sums")
                mean_square_ps[b] = moment_psum.tile([P, 1], F32, name="mean_square_ps")
            pieces = BANKS_PER_CHUNK if c == CHUNKS - 1 else 1
            width = CHUNK // pieces
            for piece in range(pieces):
                unread = unread_pool.tile([P, width], BF16, name="unread")
                first = q * CHUNK + piece * width
                nc.scalar.activation(
                    out=unread[:],
                    in_=x[b][:, first : first + width],
                    func=ACT.Square,
                    accum_out=square_sums[b][:, q + piece : q + piece + 1],
                )
                nc.tensor.matmul(
                    out=mean_square_ps[b][:],
                    lhsT=averager_2d,
                    rhs=square_sums[b][:, q + piece : q + piece + 1],
                    start=(first == 0),
                    stop=(first + width == POSITIONS),
                )

        def deviation(b):
            minus_mean[b] = stat_pool.tile([P, 1], F32, name="minus_mean")
            nc.vector.tensor_scalar(
                out=minus_mean[b][:], in0=mean_ps[b][:], scalar1=-1.0, scalar2=None, op0=ALU.mult
            )
            eps_less_square = stat_pool.tile([P, 1], F32, name="eps_less_square")
            nc.vector.scalar_tensor_tensor(
                out=eps_less_square[:],
                in0=mean_ps[b][:],
                scalar=minus_mean[b][:],
                in1=eps_col[:],
                op0=ALU.mult,
                op1=ALU.add,
            )
            nc.vector.tensor_scalar(
                out=gamma_pairs[:, b, 1:2], in0=mean_ps[b][:], scalar1=gamma_col, scalar2=-1.0, op0=ALU.mult, op1=ALU.mult
            )
            inverse_std[b] = stat_pool.tile([P, 1], F32, name="inverse_std")
            nc.scalar.activation(
                out=inverse_std[b][:],
                in_=mean_square_ps[b][:],
                func=ACT.Abs_reciprocal_sqrt,
                bias=eps_less_square[:],
            )

        def factors(b):
            gain_shift[b] = stat_pool.tile([P, 2], F32, name="gain_shift")
            nc.vector.scalar_tensor_tensor(
                out=gain_shift[b][:],
                in0=gamma_pairs[:, b, :],
                scalar=inverse_std[b][:],
                in1=zero_beta[:],
                op0=ALU.mult,
                op1=ALU.add,
            )

        def hand_over(b, q):
            handed_over[(b, q)] = handed_pool.tile([P, 2], F32, name="handed")
            nc.vector.tensor_copy(out=handed_over[(b, q)][:], in_=gain_shift[b][:])

        def normalise_on_gpsimd(b, q):
            handed = handed_over[(b, q)]
            cols = slice(q * CHUNK, (q + 1) * CHUNK)
            nc.gpsimd.tensor_scalar(
                out=x[b][:, cols],
                in0=x[b][:, cols],
                scalar1=handed[:, 0:1],
                scalar2=handed[:, 1:2],
                op0=ALU.mult,
                op1=ALU.add,
            )
            nc.sync.dma_start(out=out_rows[b, :, cols], in_=x[b][:, cols])

        def normalise_on_vector(b, q):
            cols = slice(q * CHUNK, (q + 1) * CHUNK)
            nc.vector.tensor_scalar(
                out=x[b][:, cols],
                in0=x[b][:, cols],
                scalar1=gain_shift[b][:, 0:1],
                scalar2=gain_shift[b][:, 1:2],
                op0=ALU.mult,
                op1=ALU.add,
            )
            nc.sync.dma_start(out=out_rows[b, :, cols], in_=x[b][:, cols])

        def normalise_last(b):
            gain = gain_shift[b][:, 0:1]
            shift = gain_shift[b][:, 1:2]
            first = 0
            for engine, width in LAST_PIECES:
                cols = slice(first, first + width)
                first += width
                if engine == "vector":
                    nc.vector.tensor_scalar(
                        out=x[b][:, cols], in0=x[b][:, cols], scalar1=gain, scalar2=shift, op0=ALU.mult, op1=ALU.add
                    )
                else:
                    nc.scalar.activation(
                        out=x[b][:, cols], in_=x[b][:, cols], func=ACT.Identity, scale=gain, bias=shift
                    )
                nc.sync.dma_start(out=out_rows[b, :, cols], in_=x[b][:, cols])

        w_sb = const.tile([P, K], BF16, name="w_sb")
        nc.scalar.dma_start(out=w_sb[:], in_=w_out)
        param_rows = const.tile([P, P], BF16, name="param_rows")
        nc.vector.memset(param_rows[:], 0.0)
        for row, param in enumerate((b_out, gamma, beta)):
            nc.scalar.dma_start(out=param_rows[row : row + 1, :], in_=param.rearrange("(o c) -> o c", o=1))
        for i in range(RAW_CHUNKS):
            load(i)

        eps_col = const.tile([P, 1], F32, name="eps_col")
        nc.vector.memset(eps_col[:], EPS)
        zero_beta = const.tile([P, 2], F32, name="zero_beta")
        nc.vector.memset(zero_beta[:], 0.0)
        table_warmer = const.tile([P, 1], F32, name="table_warmer")
        nc.scalar.activation(out=table_warmer[:], in_=eps_col[:], func=ACT.Abs_reciprocal_sqrt)
        identity = const.tile([P, P], F32, name="identity")
        make_identity(nc, identity[:])
        member = const.tile([P, GROUPS], F32, name="member")
        nc.vector.tensor_reduce(
            out=member[:], in_=identity[:].rearrange("k (g i) -> k g i", i=GROUP), axis=AXIS.X, op=ALU.add
        )
        averager = const.tile([P, GROUPS, GROUP], F32, name="averager")
        nc.vector.tensor_scalar(
            out=averager[:],
            in0=member[:].unsqueeze(2).to_broadcast([P, GROUPS, GROUP]),
            scalar1=1.0 / (GROUP * POSITIONS),
            scalar2=None,
            op0=ALU.mult,
        )
        averager_2d = averager[:].rearrange("k g i -> k (g i)")

        regroup(0)

        w_words = w_sb[:].bitcast(F32).rearrange("o (p u) -> o u p", u=2)
        w_turned = y_psum.tile([P, 2, CHANNELS], F32, name="w_turned", tag="y")
        for u in range(2):
            nc.tensor.transpose(w_turned[:, u, :], w_words[:, u, :], identity[:])
        w_grouped = const.tile([P, CHANNELS * PACK], BF16, name="w_grouped", align_bytes=64)
        nc.vector.tensor_copy(
            out=w_grouped[:].bitcast(F32).rearrange("p (o u) -> p o u", u=2),
            in_=w_turned[:].rearrange("p u o -> p o u"),
        )
        w_codes = const.tile([P, CHANNELS], U32, name="w_codes", align_bytes=64)
        w_scales = const.tile([P, CHANNELS], U8, name="w_scales", align_bytes=64)
        nc.vector.quantize_mx(out=w_codes[:].bitcast(FP8X4), scales=w_scales[:], in_=w_grouped[:])

        param_rows_f32 = const.tile([P, P], F32, name="param_rows_f32")
        nc.vector.tensor_copy(out=param_rows_f32[:], in_=param_rows[:])
        param_cols_ps = y_psum.tile([P, P], F32, name="param_cols_ps", tag="y")
        nc.tensor.transpose(param_cols_ps[:], param_rows_f32[:], identity[:])
        param_cols = const.tile([P, 2], F32, name="param_cols")
        nc.vector.tensor_copy(out=param_cols[:], in_=param_cols_ps[:, 0:2])
        bias_col = param_cols[:, 0:1]
        gamma_col = param_cols[:, 1:2]
        nc.vector.tensor_copy(out=zero_beta[:, 1:2], in_=param_cols_ps[:, 2:3])
        gamma_pairs = const.tile([P, SAMPLES, 2], F32, name="gamma_pairs")
        nc.vector.tensor_copy(
            out=gamma_pairs[:, :, 0:1], in_=param_cols_ps[:, 1:2].unsqueeze(1).to_broadcast([P, SAMPLES, 1])
        )

        for t in range(1, CHUNKS + 4):
            if t - 1 + RAW_CHUNKS <= CHUNKS:
                load(t - 1 + RAW_CHUNKS)
            if t < CHUNKS:
                regroup(t)
                if share_bounds(t)[0] < share_bounds(t)[1]:
                    regroup_on_gpsimd(t)
            if t >= 4 and (t - 4) % CHUNKS_PER_SAMPLE == CHUNKS_PER_SAMPLE - 1:
                factors((t - 4) // CHUNKS_PER_SAMPLE)
            b, q = divmod(t - 3 - CHUNKS_PER_SAMPLE, CHUNKS_PER_SAMPLE)
            on_gpsimd = 0 <= b < SAMPLES - 1 and t - 2 < CHUNKS
            if on_gpsimd:
                hand_over(b, q)
            if t - 1 < CHUNKS:
                quantise(t - 1)
                multiply(t - 1)
            if t >= 3 and (t - 3) % CHUNKS_PER_SAMPLE == CHUNKS_PER_SAMPLE - 1:
                deviation((t - 3) // CHUNKS_PER_SAMPLE)
            if on_gpsimd:
                normalise_on_gpsimd(b, q)
            if 0 <= t - 2 < CHUNKS:
                residual(t - 2)
                squares(t - 2)
            if t - 2 == CHUNKS - 1:
                normalise_on_vector(SAMPLES - 2, CHUNKS_PER_SAMPLE - 1)
        normalise_last(SAMPLES - 1)
